import numpy as np
import ml_dtypes


def mxq(x, axis, fmt="e4m3"):
    dtype, down = {"e4m3": (ml_dtypes.float8_e4m3fn, 7), "e5m2": (ml_dtypes.float8_e5m2, 14)}[fmt]
    v = np.moveaxis(np.asarray(x, np.float32).astype(ml_dtypes.bfloat16).astype(np.float64), axis, -1)
    blocks = v.reshape(v.shape[:-1] + (-1, 32))
    amax = np.abs(blocks).max(-1, keepdims=True)
    byte = np.maximum(np.where(amax > 0, np.frexp(amax)[1] - 1 + 127, 0) - down, 1)
    scale = np.exp2(byte - 127.0)
    codes = (blocks / scale).astype(np.float32).astype(dtype).astype(np.float64)
    return np.moveaxis((codes * scale).reshape(v.shape), -1, axis)


WIDE = False


def mx_kscale(k):
    if not WIDE:
        return np.ones(k)
    levels = np.array([10, -10, 5, -5, 0])
    a = np.random.permutation(np.resize(levels, k // 512 * 4)).reshape(k // 512, 4)
    idx = np.arange(k)
    return np.exp2(a[idx // 512, idx % 128 // 32])


BF16 = ml_dtypes.bfloat16


def bf(x):
    return np.asarray(x, np.float32).astype(BF16)


def f64(x):
    return np.asarray(x).astype(np.float64)


B, L, E, QH, KVH, D, FFN = 2, 256, 1024, 8, 2, 128, 4096
KV = KVH * D
EPS = 1.1920928955078125e-07


def rmsnorm(x, w):
    return x / np.sqrt(np.mean(x * x, axis=-1, keepdims=True) + EPS) * w


def setup_inputs():
    s, t = mx_kscale(FFN), mx_kscale(E)
    return {"ffn_act": bf(np.random.standard_normal((B, L, FFN)) * 0.6 * s),
            "wd": bf(np.random.standard_normal((FFN, E)) / np.sqrt(FFN) / s[:, None]),
            "residual": bf(np.random.standard_normal((B, L, E)) * 1.1),
            "ln1_w": bf((1.0 + 0.1 * np.random.standard_normal(E)) * t),
            "wk": bf(np.random.standard_normal((E, KV)) / np.sqrt(E) / t[:, None]),
            "wv": bf(np.random.standard_normal((E, KV)) / np.sqrt(E) / t[:, None])}


def reference(ffn_act, wd, residual, ln1_w, wk, wv):
    x_out = (mxq(f64(ffn_act), 2, "e4m3") @ mxq(f64(wd), 0, "e4m3")) + f64(residual)
    hq = mxq(rmsnorm(x_out, f64(ln1_w)), 2, "e4m3")
    k_out = (hq @ mxq(f64(wk), 0, "e4m3")).reshape(B, L, KV)
    v_out = (hq @ mxq(f64(wv), 0, "e4m3")).reshape(B, L, KV)
    return x_out, k_out, v_out

@@ -1,0 +1,244 @@
+from contextlib import ExitStack
+
+import concourse.mybir as mybir
+from concourse.masks import make_identity
+
+F32 = mybir.dt.float32
+BF16 = mybir.dt.bfloat16
+U32 = mybir.dt.uint32
+U8 = mybir.dt.uint8
+FP8X4 = mybir.dt.float8_e4m3fn_x4
+ALU = mybir.AluOpType
+ACT = mybir.ActivationFunctionType
+
+P = 128
+PACK = 4
+K_PASS = P * PACK
+BANK = 512
+BANKS = 8
+
+TOKENS = 512
+FFN = 4096
+E = 1024
+KV = 256
+EPS = 2.0 ** -23
+
+TOKEN_TILES = TOKENS // P
+FFN_PASSES = FFN // K_PASS
+E_PASSES = E // K_PASS
+E_HALVES = E // BANK
+PASSES_PER_BANK = 2
+PASSES_PER_QUANTISE = 4
+RUN = 4
+WD_BUFS = 6
+
+FLOPS = 2 * TOKENS * FFN * E + 2 * TOKENS * E * 2 * KV
+
+
+def regroup(copy, four_rows, grouped):
+    copy(
+        out=grouped.rearrange("p (c i) t -> p c t i", i=RUN),
+        in_=four_rows.rearrange("p t (c i) -> p c t i", i=RUN),
+    )
+
+
+def tile_textencoderblock_pc_kernel(tc, ffn_act, wd, residual, ln1_w, wk, wv, out_0, out_1, out_2):
+    nc = tc.nc
+    act_rows = ffn_act.flatten_outer_dims()
+    res_rows = residual.flatten_outer_dims()
+    x_rows = out_0.flatten_outer_dims()
+    k_rows = out_1.flatten_outer_dims()
+    v_rows = out_2.flatten_outer_dims()
+
+    with ExitStack() as ctx:
+        keep = ctx.enter_context(tc.tile_pool(name="keep", bufs=1))
+        act_pool = ctx.enter_context(tc.tile_pool(name="act", bufs=2))
+        wd_pool = ctx.enter_context(tc.tile_pool(name="wd", bufs=3))
+        tail = ctx.enter_context(tc.tile_pool(name="tail", bufs=2))
+        psum = ctx.enter_context(tc.psum_pool(name="psum", bufs=BANKS))
+        ctx.enter_context(tc.manual_schedule())
+
+        gain_rows = keep.tile([P, E], BF16)
+        nc.vector.memset(gain_rows[:], 0.0)
+        ones = keep.tile([P, P], BF16)
+        nc.vector.memset(ones[:], 1.0)
+        one_col = keep.tile([P, 1], F32)
+        nc.vector.memset(one_col[:], 1.0)
+        warm_col = keep.tile([P, 1], F32)
+        nc.scalar.activation(out=warm_col[:], in_=one_col[:], func=ACT.Sqrt)
+        ident_f32 = keep.tile([P, P], F32)
+        make_identity(nc, ident_f32[:])
+        ident_bf16 = keep.tile([P, P], BF16)
+        make_identity(nc, ident_bf16[:])
+
+        act_raw = []
+        for m in range(TOKEN_TILES):
+            raw = act_pool.tile([P, FFN], BF16, tag="act_raw", bufs=TOKEN_TILES, name="act_raw_%d" % m)
+            nc.sync.dma_start(out=raw[:], in_=act_rows[m * P : (m + 1) * P, :])
+            act_raw.append(raw)
+            if m == 0:
+                nc.sync.dma_start(out=gain_rows[0:1, :], in_=ln1_w.rearrange("(o e) -> o e", o=1))
+
+        wd_raw = {}
+
+        def load_wd(c):
+            raw = wd_pool.tile([P, PACK, E], BF16, tag="wd_raw", bufs=WD_BUFS, name="wd_raw_%d" % c)
+            nc.sync.dma_start(
+                out=raw[:].rearrange("p (u e) n -> p u e n", u=2),
+                in_=wd[c * K_PASS : (c + 1) * K_PASS, :].rearrange("(u p e) n -> p u e n", u=2, e=2),
+            )
+            wd_raw[c] = raw
+
+        for c in range(WD_BUFS):
+            load_wd(c)
+
+        act_codes = keep.tile([P, TOKEN_TILES, FFN_PASSES, P], U32, align_bytes=64)
+        act_scales = keep.tile([P, TOKEN_TILES, FFN_PASSES, P], U8, align_bytes=64)
+
+        def prepare_act(m):
+            act_words = act_raw[m][:].bitcast(F32)
+            act_grouped = act_pool.tile([P, FFN_PASSES, P * PACK], BF16, tag="act_grouped", align_bytes=64)
+            grouped_words = act_grouped[:].bitcast(F32).rearrange("p g (r u) -> p g r u", u=2)
+            for g0 in range(0, FFN_PASSES, PASSES_PER_BANK):
+                words_t = psum.tile([P, PASSES_PER_BANK, 2, P], F32, tag="bank")
+                for j in range(PASSES_PER_BANK):
+                    for u in range(2):
+                        w0 = (g0 + j) * 2 * P + u * P
+                        nc.tensor.transpose(words_t[:, j, u, :], act_words[:, w0 : w0 + P], ident_f32[:])
+                copy = nc.vector.tensor_copy if g0 + PASSES_PER_BANK == FFN_PASSES else nc.scalar.copy
+                copy(
+                    out=grouped_words[:, g0 : g0 + PASSES_PER_BANK],
+                    in_=words_t[:].rearrange("p g u r -> p g r u"),
+                )
+            for g0 in range(0, FFN_PASSES, PASSES_PER_QUANTISE):
+                gs = slice(g0, g0 + PASSES_PER_QUANTISE)
+                nc.vector.quantize_mx(
+                    out=act_codes[:, m, gs, :].bitcast(FP8X4).rearrange("p g r -> p (g r)"),
+                    scales=act_scales[:, m, gs, :].rearrange("p g r -> p (g r)"),
+                    in_=act_grouped[:, gs, :].rearrange("p g c -> p (g c)"),
+                )
+
+        gain_all = keep.tile([P, E], BF16)
+        for m in range(TOKEN_TILES):
+            prepare_act(m)
+            if m == 0:
+                gain_ps = psum.tile([P, E], BF16, tag="bank")
+                for half in range(E_HALVES):
+                    cols = slice(half * BANK, (half + 1) * BANK)
+                    nc.tensor.matmul(out=gain_ps[:, cols], lhsT=ones[:], rhs=gain_rows[:, cols], start=True, stop=True)
+                nc.vector.tensor_copy(out=gain_all[:], in_=gain_ps[:])
+
+        acc = {}
+        for m in range(TOKEN_TILES):
+            for half in range(E_HALVES):
+                acc[(m, half)] = psum.tile([P, BANK], F32, tag="bank", name="acc_%d_%d" % (m, half))
+
+        wd_grouped = {}
+
+        def quantise_and_multiply(c, half):
+            codes = wd_pool.tile([P, BANK], U32, tag="wd_codes", align_bytes=64)
+            scales = wd_pool.tile([P, BANK], U8, tag="wd_scales", align_bytes=64)
+            nc.vector.quantize_mx(
+                out=codes[:].bitcast(FP8X4),
+                scales=scales[:],
+                in_=wd_grouped[(c, half)][:].rearrange("p n t -> p (n t)"),
+            )
+            for m in range(TOKEN_TILES):
+                nc.tensor.matmul_mx(
+                    out=acc[(m, half)][:],
+                    lhsT=act_codes[:, m, c, :].bitcast(FP8X4),
+                    lhsT_scale=act_scales[:, m, c, :],
+                    rhs=codes[:].bitcast(FP8X4),
+                    rhs_scale=scales[:],
+                    start=(c == 0),
+                    stop=(c == FFN_PASSES - 1),
+                )
+
+        for c in range(FFN_PASSES):
+            for half, copy in enumerate((nc.vector.tensor_copy, nc.scalar.copy)):
+                grouped = wd_pool.tile([P, BANK, PACK], BF16, tag="wd_grouped_%d" % half, align_bytes=64, name="wd_grouped_%d_%d" % (c, half))
+                regroup(copy, wd_raw[c][:, :, half * BANK : (half + 1) * BANK], grouped[:])
+                wd_grouped[(c, half)] = grouped
+            if c + WD_BUFS < FFN_PASSES:
+                load_wd(c + WD_BUFS)
+            if c > 0:
+                quantise_and_multiply(c - 1, 1)
+            quantise_and_multiply(c, 0)
+
+        wkv_raw = keep.tile([P, E_PASSES, PACK, 2 * KV], BF16)
+        nc.sync.dma_start(out=wkv_raw[:, :, :, 0:KV], in_=wk.rearrange("(g t p) n -> p g t n", t=PACK, p=P))
+        nc.sync.dma_start(out=wkv_raw[:, :, :, KV : 2 * KV], in_=wv.rearrange("(g t p) n -> p g t n", t=PACK, p=P))
+        res_all = keep.tile([P, TOKEN_TILES, E], BF16)
+        for m in range(TOKEN_TILES):
+            nc.sync.dma_start(out=res_all[:, m, :], in_=res_rows[m * P : (m + 1) * P, :])
+
+        quantise_and_multiply(FFN_PASSES - 1, 1)
+
+        wkv_grouped = keep.tile([P, E_PASSES, 2 * KV, PACK], BF16, align_bytes=64)
+        for g in range(E_PASSES):
+            regroup(nc.scalar.copy, wkv_raw[:, g], wkv_grouped[:, g])
+
+        x_sb = []
+        rms = []
+        for m in range(TOKEN_TILES):
+            x = tail.tile([P, E], F32, tag="x", bufs=TOKEN_TILES, name="x_%d" % m)
+            for half in range(E_HALVES):
+                cols = slice(half * BANK, (half + 1) * BANK)
+                nc.vector.tensor_tensor(out=x[:, cols], in0=acc[(m, half)][:], in1=res_all[:, m, cols], op=ALU.add)
+            nc.sync.dma_start(out=x_rows[m * P : (m + 1) * P, :], in_=x[:])
+            squares = tail.tile([P, E], BF16, tag="squares", bufs=TOKEN_TILES)
+            sum_sq = tail.tile([P, 1], F32, tag="sum_sq", bufs=TOKEN_TILES)
+            nc.scalar.activation(out=squares[:], in_=x[:], func=ACT.Square, accum_out=sum_sq[:])
+            root = tail.tile([P, 1], F32, tag="rms", bufs=TOKEN_TILES, name="rms_%d" % m)
+            nc.scalar.activation(out=root[:], in_=sum_sq[:], func=ACT.Sqrt, scale=1.0 / E, bias=EPS)
+            x_sb.append(x)
+            rms.append(root)
+
+        h_grouped = []
+        for m in range(TOKEN_TILES):
+            inv_rms = tail.tile([P, 1], F32, tag="inv_rms", bufs=TOKEN_TILES)
+            nc.vector.reciprocal(out=inv_rms[:], in_=rms[m][:])
+            h = tail.tile([P, E], BF16, tag="h")
+            nc.vector.scalar_tensor_tensor(
+                out=h[:], in0=x_sb[m][:], scalar=inv_rms[:], in1=gain_all[:], op0=ALU.mult, op1=ALU.mult
+            )
+            h_t = psum.tile([P, E_PASSES, PACK, P], BF16, tag="bank")
+            for g in range(E_PASSES):
+                for t in range(PACK):
+                    e0 = g * K_PASS + t * P
+                    nc.tensor.transpose(h_t[:, g, t, :], h[:, e0 : e0 + P], ident_bf16[:])
+            grouped = tail.tile([P, E_PASSES, P, PACK], BF16, tag="h_grouped", bufs=TOKEN_TILES, align_bytes=64, name="h_grouped_%d" % m)
+            nc.scalar.copy(out=grouped[:], in_=h_t[:].rearrange("p g t r -> p g r t"))
+            h_grouped.append(grouped)
+
+        wkv_codes = keep.tile([P, E_PASSES, 2 * KV], U32, align_bytes=64)
+        wkv_scales = keep.tile([P, E_PASSES, 2 * KV], U8, align_bytes=64)
+        for g in range(E_PASSES):
+            nc.vector.quantize_mx(
+                out=wkv_codes[:, g, :].bitcast(FP8X4),
+                scales=wkv_scales[:, g, :],
+                in_=wkv_grouped[:, g].rearrange("p n t -> p (n t)"),
+            )
+        for m in range(TOKEN_TILES):
+            h_codes = tail.tile([P, E_PASSES, P], U32, tag="h_codes", align_bytes=64)
+            h_scales = tail.tile([P, E_PASSES, P], U8, tag="h_scales", align_bytes=64)
+            nc.vector.quantize_mx(
+                out=h_codes[:].bitcast(FP8X4).rearrange("p g r -> p (g r)"),
+                scales=h_scales[:].rearrange("p g r -> p (g r)"),
+                in_=h_grouped[m][:].rearrange("p g r t -> p (g r t)"),
+            )
+            kv_ps = psum.tile([P, 2 * KV], F32, tag="bank")
+            for g in range(E_PASSES):
+                nc.tensor.matmul_mx(
+                    out=kv_ps[:],
+                    lhsT=h_codes[:, g, :].bitcast(FP8X4),
+                    lhsT_scale=h_scales[:, g, :],
+                    rhs=wkv_codes[:, g, :].bitcast(FP8X4),
+                    rhs_scale=wkv_scales[:, g, :],
+                    start=(g == 0),
+                    stop=(g == E_PASSES - 1),
+                )
+            kv = tail.tile([P, 2 * KV], F32, tag="kv")
+            nc.scalar.copy(out=kv[:], in_=kv_ps[:])
+            nc.sync.dma_start(out=k_rows[m * P : (m + 1) * P, :], in_=kv[:, 0:KV])
+            nc.sync.dma_start(out=v_rows[m * P : (m + 1) * P, :], in_=kv[:, KV : 2 * KV])

@@ -68,8 +68,6 @@ def tile_textencoderblock_pc_kernel(tc, ffn_act, wd, residual, ln1_w, wk, wv, ou
         nc.scalar.activation(out=warm_col[:], in_=one_col[:], func=ACT.Sqrt)
         ident_f32 = keep.tile([P, P], F32)
         make_identity(nc, ident_f32[:])
-        ident_bf16 = keep.tile([P, P], BF16)
-        make_identity(nc, ident_bf16[:])
 
         act_raw = []
         for m in range(TOKEN_TILES):
@@ -165,9 +163,14 @@ def tile_textencoderblock_pc_kernel(tc, ffn_act, wd, residual, ln1_w, wk, wv, ou
                 quantise_and_multiply(c - 1, 1)
             quantise_and_multiply(c, 0)
 
-        wkv_raw = keep.tile([P, E_PASSES, PACK, 2 * KV], BF16)
-        nc.sync.dma_start(out=wkv_raw[:, :, :, 0:KV], in_=wk.rearrange("(g t p) n -> p g t n", t=PACK, p=P))
-        nc.sync.dma_start(out=wkv_raw[:, :, :, KV : 2 * KV], in_=wv.rearrange("(g t p) n -> p g t n", t=PACK, p=P))
+        wkv_raw = []
+        for name, weight in (("wk_raw", wk), ("wv_raw", wv)):
+            raw = keep.tile([P, E_PASSES, PACK, KV], BF16, name=name)
+            nc.sync.dma_start(
+                out=raw[:].rearrange("p g (u j) n -> p (g u) j n", j=2),
+                in_=weight.rearrange("(v p j) n -> p v j n", p=P, j=2),
+            )
+            wkv_raw.append(raw)
         res_all = keep.tile([P, TOKEN_TILES, E], BF16)
         for m in range(TOKEN_TILES):
             nc.sync.dma_start(out=res_all[:, m, :], in_=res_rows[m * P : (m + 1) * P, :])
@@ -176,7 +179,8 @@ def tile_textencoderblock_pc_kernel(tc, ffn_act, wd, residual, ln1_w, wk, wv, ou
 
         wkv_grouped = keep.tile([P, E_PASSES, 2 * KV, PACK], BF16, align_bytes=64)
         for g in range(E_PASSES):
-            regroup(nc.scalar.copy, wkv_raw[:, g], wkv_grouped[:, g])
+            for i, raw in enumerate(wkv_raw):
+                regroup(nc.scalar.copy, raw[:, g], wkv_grouped[:, g, i * KV : (i + 1) * KV])
 
         x_sb = []
         rms = []
@@ -186,7 +190,7 @@ def tile_textencoderblock_pc_kernel(tc, ffn_act, wd, residual, ln1_w, wk, wv, ou
                 cols = slice(half * BANK, (half + 1) * BANK)
                 nc.vector.tensor_tensor(out=x[:, cols], in0=acc[(m, half)][:], in1=res_all[:, m, cols], op=ALU.add)
             nc.sync.dma_start(out=x_rows[m * P : (m + 1) * P, :], in_=x[:])
-            squares = tail.tile([P, E], BF16, tag="squares", bufs=TOKEN_TILES)
+            squares = tail.tile([P, E], BF16, tag="squares")
             sum_sq = tail.tile([P, 1], F32, tag="sum_sq", bufs=TOKEN_TILES)
             nc.scalar.activation(out=squares[:], in_=x[:], func=ACT.Square, accum_out=sum_sq[:])
             root = tail.tile([P, 1], F32, tag="rms", bufs=TOKEN_TILES, name="rms_%d" % m)
@@ -202,13 +206,17 @@ def tile_textencoderblock_pc_kernel(tc, ffn_act, wd, residual, ln1_w, wk, wv, ou
             nc.vector.scalar_tensor_tensor(
                 out=h[:], in0=x_sb[m][:], scalar=inv_rms[:], in1=gain_all[:], op0=ALU.mult, op1=ALU.mult
             )
-            h_t = psum.tile([P, E_PASSES, PACK, P], BF16, tag="bank")
+            h_words = h[:].bitcast(F32)
+            h_t = psum.tile([P, E_PASSES, 2, P], F32, tag="bank")
             for g in range(E_PASSES):
-                for t in range(PACK):
-                    e0 = g * K_PASS + t * P
-                    nc.tensor.transpose(h_t[:, g, t, :], h[:, e0 : e0 + P], ident_bf16[:])
-            grouped = tail.tile([P, E_PASSES, P, PACK], BF16, tag="h_grouped", bufs=TOKEN_TILES, align_bytes=64, name="h_grouped_%d" % m)
-            nc.scalar.copy(out=grouped[:], in_=h_t[:].rearrange("p g t r -> p g r t"))
+                for u in range(2):
+                    w0 = g * 2 * P + u * P
+                    nc.tensor.transpose(h_t[:, g, u, :], h_words[:, w0 : w0 + P], ident_f32[:])
+            grouped = tail.tile([P, E_PASSES, P * PACK], BF16, tag="h_grouped", bufs=TOKEN_TILES, align_bytes=64, name="h_grouped_%d" % m)
+            nc.scalar.copy(
+                out=grouped[:].bitcast(F32).rearrange("p g (r u) -> p g r u", u=2),
+                in_=h_t[:].rearrange("p g u r -> p g r u"),
+            )
             h_grouped.append(grouped)
 
         wkv_codes = keep.tile([P, E_PASSES, 2 * KV], U32, align_bytes=64)
@@ -220,12 +228,12 @@ def tile_textencoderblock_pc_kernel(tc, ffn_act, wd, residual, ln1_w, wk, wv, ou
                 in_=wkv_grouped[:, g].rearrange("p n t -> p (n t)"),
             )
         for m in range(TOKEN_TILES):
-            h_codes = tail.tile([P, E_PASSES, P], U32, tag="h_codes", align_bytes=64)
-            h_scales = tail.tile([P, E_PASSES, P], U8, tag="h_scales", align_bytes=64)
+            h_codes = tail.tile([P, E_PASSES, P], U32, tag="h_codes", bufs=TOKEN_TILES, align_bytes=64)
+            h_scales = tail.tile([P, E_PASSES, P], U8, tag="h_scales", bufs=TOKEN_TILES, align_bytes=64)
             nc.vector.quantize_mx(
                 out=h_codes[:].bitcast(FP8X4).rearrange("p g r -> p (g r)"),
                 scales=h_scales[:].rearrange("p g r -> p (g r)"),
-                in_=h_grouped[m][:].rearrange("p g r t -> p (g r t)"),
+                in_=h_grouped[m][:].rearrange("p g c -> p (g c)"),
             )
             kv_ps = psum.tile([P, 2 * KV], F32, tag="bank")
             for g in range(E_PASSES):
@@ -238,7 +246,7 @@ def tile_textencoderblock_pc_kernel(tc, ffn_act, wd, residual, ln1_w, wk, wv, ou
                     start=(g == 0),
                     stop=(g == E_PASSES - 1),
                 )
-            kv = tail.tile([P, 2 * KV], F32, tag="kv")
+            kv = tail.tile([P, 2 * KV], F32, tag="kv", bufs=TOKEN_TILES)
             nc.scalar.copy(out=kv[:], in_=kv_ps[:])
             nc.sync.dma_start(out=k_rows[m * P : (m + 1) * P, :], in_=kv[:, 0:KV])
             nc.sync.dma_start(out=v_rows[m * P : (m + 1) * P, :], in_=kv[:, KV : 2 * KV])

@@ -65,7 +65,7 @@ def tile_textencoderblock_pc_kernel(tc, ffn_act, wd, residual, ln1_w, wk, wv, ou
         one_col = keep.tile([P, 1], F32)
         nc.vector.memset(one_col[:], 1.0)
         warm_col = keep.tile([P, 1], F32)
-        nc.scalar.activation(out=warm_col[:], in_=one_col[:], func=ACT.Sqrt)
+        nc.scalar.activation(out=warm_col[:], in_=one_col[:], func=ACT.Abs_reciprocal_sqrt)
         ident_f32 = keep.tile([P, P], F32)
         make_identity(nc, ident_f32[:])
 
@@ -81,10 +81,20 @@ def tile_textencoderblock_pc_kernel(tc, ffn_act, wd, residual, ln1_w, wk, wv, ou
 
         def load_wd(c):
             raw = wd_pool.tile([P, PACK, E], BF16, tag="wd_raw", bufs=WD_BUFS, name="wd_raw_%d" % c)
-            nc.sync.dma_start(
-                out=raw[:].rearrange("p (u e) n -> p u e n", u=2),
-                in_=wd[c * K_PASS : (c + 1) * K_PASS, :].rearrange("(u p e) n -> p u e n", u=2, e=2),
-            )
+            rows = wd[c * K_PASS : (c + 1) * K_PASS, :]
+            if c < FFN_PASSES - 1:
+                nc.sync.dma_start(
+                    out=raw[:].rearrange("p (u e) n -> p u e n", u=2),
+                    in_=rows.rearrange("(u p e) n -> p u e n", u=2, e=2),
+                )
+            else:
+                for half in range(E_HALVES):
+                    cols = slice(half * BANK, (half + 1) * BANK)
+                    for u in range(2):
+                        nc.sync.dma_start(
+                            out=raw[:, 2 * u : 2 * u + 2, cols],
+                            in_=rows[u * 2 * P : (u + 1) * 2 * P, cols].rearrange("(p e) n -> p e n", e=2),
+                        )
             wd_raw[c] = raw
 
         for c in range(WD_BUFS):
@@ -152,59 +162,89 @@ def tile_textencoderblock_pc_kernel(tc, ffn_act, wd, residual, ln1_w, wk, wv, ou
                     stop=(c == FFN_PASSES - 1),
                 )
 
-        for c in range(FFN_PASSES):
+        def grouped_tile(c, half):
+            wd_grouped[(c, half)] = wd_pool.tile([P, BANK, PACK], BF16, tag="wd_grouped_%d" % half, align_bytes=64, name="wd_grouped_%d_%d" % (c, half))
+            return wd_grouped[(c, half)]
+
+        for c in range(FFN_PASSES - 1):
             for half, copy in enumerate((nc.vector.tensor_copy, nc.scalar.copy)):
-                grouped = wd_pool.tile([P, BANK, PACK], BF16, tag="wd_grouped_%d" % half, align_bytes=64, name="wd_grouped_%d_%d" % (c, half))
-                regroup(copy, wd_raw[c][:, :, half * BANK : (half + 1) * BANK], grouped[:])
-                wd_grouped[(c, half)] = grouped
+                regroup(copy, wd_raw[c][:, :, half * BANK : (half + 1) * BANK], grouped_tile(c, half)[:])
             if c + WD_BUFS < FFN_PASSES:
                 load_wd(c + WD_BUFS)
             if c > 0:
                 quantise_and_multiply(c - 1, 1)
             quantise_and_multiply(c, 0)
+        c = FFN_PASSES - 1
+        regroup(nc.vector.tensor_copy, wd_raw[c][:, :, 0:BANK], grouped_tile(c, 0)[:])
+        quantise_and_multiply(c - 1, 1)
+        quantise_and_multiply(c, 0)
+        last = grouped_tile(c, 1)
+        shared = BANK // 2
+        regroup(nc.vector.tensor_copy, wd_raw[c][:, :, BANK : BANK + shared], last[:, 0:shared, :])
+        regroup(nc.scalar.copy, wd_raw[c][:, :, BANK + shared : E], last[:, shared:BANK, :])
 
         wkv_raw = []
-        for name, weight in (("wk_raw", wk), ("wv_raw", wv)):
-            raw = keep.tile([P, E_PASSES, PACK, KV], BF16, name=name)
+        res_all = keep.tile([P, TOKEN_TILES, E], BF16)
+        for i, weight in enumerate((wk, wv)):
+            raw = keep.tile([P, E_PASSES, PACK, KV], BF16, name="w%s_raw" % "kv"[i])
             nc.sync.dma_start(
                 out=raw[:].rearrange("p g (u j) n -> p (g u) j n", j=2),
                 in_=weight.rearrange("(v p j) n -> p v j n", p=P, j=2),
             )
             wkv_raw.append(raw)
-        res_all = keep.tile([P, TOKEN_TILES, E], BF16)
-        for m in range(TOKEN_TILES):
-            nc.sync.dma_start(out=res_all[:, m, :], in_=res_rows[m * P : (m + 1) * P, :])
+            for m in (2 * i, 2 * i + 1):
+                nc.sync.dma_start(out=res_all[:, m, :], in_=res_rows[m * P : (m + 1) * P, :])
 
         quantise_and_multiply(FFN_PASSES - 1, 1)
 
         wkv_grouped = keep.tile([P, E_PASSES, 2 * KV, PACK], BF16, align_bytes=64)
-        for g in range(E_PASSES):
-            for i, raw in enumerate(wkv_raw):
-                regroup(nc.scalar.copy, raw[:, g], wkv_grouped[:, g, i * KV : (i + 1) * KV])
+
+        def regroup_wkv(g, i):
+            regroup(nc.scalar.copy, wkv_raw[i][:, g], wkv_grouped[:, g, i * KV : (i + 1) * KV])
+
+        regroup_wkv(0, 0)
+        regroup_wkv(1, 0)
+        regroup_wkv(0, 1)
 
         x_sb = []
-        rms = []
-        for m in range(TOKEN_TILES):
-            x = tail.tile([P, E], F32, tag="x", bufs=TOKEN_TILES, name="x_%d" % m)
-            for half in range(E_HALVES):
-                cols = slice(half * BANK, (half + 1) * BANK)
-                nc.vector.tensor_tensor(out=x[:, cols], in0=acc[(m, half)][:], in1=res_all[:, m, cols], op=ALU.add)
-            nc.sync.dma_start(out=x_rows[m * P : (m + 1) * P, :], in_=x[:])
+        sum_sq = []
+        inv_rms = []
+
+        def add_residual(m, half):
+            if half == 0:
+                x_sb.append(tail.tile([P, E], F32, tag="x", bufs=TOKEN_TILES, name="x_%d" % m))
+            cols = slice(half * BANK, (half + 1) * BANK)
+            nc.vector.tensor_tensor(out=x_sb[m][:, cols], in0=acc[(m, half)][:], in1=res_all[:, m, cols], op=ALU.add)
+
+        def measure(m):
+            nc.sync.dma_start(out=x_rows[m * P : (m + 1) * P, :], in_=x_sb[m][:])
             squares = tail.tile([P, E], BF16, tag="squares")
-            sum_sq = tail.tile([P, 1], F32, tag="sum_sq", bufs=TOKEN_TILES)
-            nc.scalar.activation(out=squares[:], in_=x[:], func=ACT.Square, accum_out=sum_sq[:])
-            root = tail.tile([P, 1], F32, tag="rms", bufs=TOKEN_TILES, name="rms_%d" % m)
-            nc.scalar.activation(out=root[:], in_=sum_sq[:], func=ACT.Sqrt, scale=1.0 / E, bias=EPS)
-            x_sb.append(x)
-            rms.append(root)
+            total = tail.tile([P, 1], F32, tag="sum_sq", bufs=TOKEN_TILES, name="sum_sq_%d" % m)
+            nc.scalar.activation(out=squares[:], in_=x_sb[m][:], func=ACT.Square, accum_out=total[:])
+            sum_sq.append(total)
+
+        def invert(m):
+            inv = tail.tile([P, 1], F32, tag="inv_rms", bufs=TOKEN_TILES, name="inv_rms_%d" % m)
+            nc.scalar.activation(out=inv[:], in_=sum_sq[m][:], func=ACT.Abs_reciprocal_sqrt, scale=1.0 / E, bias=EPS)
+            inv_rms.append(inv)
+
+        for m in (0, 2):
+            for half in range(E_HALVES):
+                add_residual(m, half)
+                add_residual(m + 1, half)
+            for i in (m, m + 1):
+                measure(i)
+                if i > 0:
+                    invert(i - 1)
+        invert(TOKEN_TILES - 1)
+        regroup_wkv(1, 1)
 
         h_grouped = []
-        for m in range(TOKEN_TILES):
-            inv_rms = tail.tile([P, 1], F32, tag="inv_rms", bufs=TOKEN_TILES)
-            nc.vector.reciprocal(out=inv_rms[:], in_=rms[m][:])
+
+        def normalise(m):
             h = tail.tile([P, E], BF16, tag="h")
             nc.vector.scalar_tensor_tensor(
-                out=h[:], in0=x_sb[m][:], scalar=inv_rms[:], in1=gain_all[:], op0=ALU.mult, op1=ALU.mult
+                out=h[:], in0=x_sb[m][:], scalar=inv_rms[m][:], in1=gain_all[:], op0=ALU.mult, op1=ALU.mult
             )
             h_words = h[:].bitcast(F32)
             h_t = psum.tile([P, E_PASSES, 2, P], F32, tag="bank")
@@ -221,20 +261,28 @@ def tile_textencoderblock_pc_kernel(tc, ffn_act, wd, residual, ln1_w, wk, wv, ou
 
         wkv_codes = keep.tile([P, E_PASSES, 2 * KV], U32, align_bytes=64)
         wkv_scales = keep.tile([P, E_PASSES, 2 * KV], U8, align_bytes=64)
-        for g in range(E_PASSES):
+
+        def quantise_wkv(g):
             nc.vector.quantize_mx(
                 out=wkv_codes[:, g, :].bitcast(FP8X4),
                 scales=wkv_scales[:, g, :],
                 in_=wkv_grouped[:, g].rearrange("p n t -> p (n t)"),
             )
-        for m in range(TOKEN_TILES):
-            h_codes = tail.tile([P, E_PASSES, P], U32, tag="h_codes", bufs=TOKEN_TILES, align_bytes=64)
-            h_scales = tail.tile([P, E_PASSES, P], U8, tag="h_scales", bufs=TOKEN_TILES, align_bytes=64)
+
+        h_quantised = []
+
+        def quantise_h(m):
+            codes = tail.tile([P, E_PASSES, P], U32, tag="h_codes", bufs=TOKEN_TILES, align_bytes=64, name="h_codes_%d" % m)
+            scales = tail.tile([P, E_PASSES, P], U8, tag="h_scales", bufs=TOKEN_TILES, align_bytes=64, name="h_scales_%d" % m)
             nc.vector.quantize_mx(
-                out=h_codes[:].bitcast(FP8X4).rearrange("p g r -> p (g r)"),
-                scales=h_scales[:].rearrange("p g r -> p (g r)"),
+                out=codes[:].bitcast(FP8X4).rearrange("p g r -> p (g r)"),
+                scales=scales[:].rearrange("p g r -> p (g r)"),
                 in_=h_grouped[m][:].rearrange("p g c -> p (g c)"),
             )
+            h_quantised.append((codes, scales))
+
+        def project(m):
+            h_codes, h_scales = h_quantised[m]
             kv_ps = psum.tile([P, 2 * KV], F32, tag="bank")
             for g in range(E_PASSES):
                 nc.tensor.matmul_mx(
@@ -250,3 +298,18 @@ def tile_textencoderblock_pc_kernel(tc, ffn_act, wd, residual, ln1_w, wk, wv, ou
             nc.scalar.copy(out=kv[:], in_=kv_ps[:])
             nc.sync.dma_start(out=k_rows[m * P : (m + 1) * P, :], in_=kv[:, 0:KV])
             nc.sync.dma_start(out=v_rows[m * P : (m + 1) * P, :], in_=kv[:, KV : 2 * KV])
+
+        normalise(0)
+        normalise(1)
+        quantise_wkv(0)
+        normalise(2)
+        quantise_wkv(1)
+        quantise_h(0)
+        project(0)
+        normalise(3)
+        quantise_h(1)
+        project(1)
+        quantise_h(2)
+        project(2)
+        quantise_h(3)
+        project(3)

@@ -103,6 +103,8 @@ def tile_textencoderblock_pc_kernel(tc, ffn_act, wd, residual, ln1_w, wk, wv, ou
         act_codes = keep.tile([P, TOKEN_TILES, FFN_PASSES, P], U32, align_bytes=64)
         act_scales = keep.tile([P, TOKEN_TILES, FFN_PASSES, P], U8, align_bytes=64)
 
+        grouped_acts = []
+
         def prepare_act(m):
             act_words = act_raw[m][:].bitcast(F32)
             act_grouped = act_pool.tile([P, FFN_PASSES, P * PACK], BF16, tag="act_grouped", align_bytes=64)
@@ -113,28 +115,32 @@ def tile_textencoderblock_pc_kernel(tc, ffn_act, wd, residual, ln1_w, wk, wv, ou
                     for u in range(2):
                         w0 = (g0 + j) * 2 * P + u * P
                         nc.tensor.transpose(words_t[:, j, u, :], act_words[:, w0 : w0 + P], ident_f32[:])
-                copy = nc.vector.tensor_copy if g0 + PASSES_PER_BANK == FFN_PASSES else nc.scalar.copy
-                copy(
+                nc.scalar.copy(
                     out=grouped_words[:, g0 : g0 + PASSES_PER_BANK],
                     in_=words_t[:].rearrange("p g u r -> p g r u"),
                 )
+            grouped_acts.append(act_grouped)
+
+        def quantise_act(m):
             for g0 in range(0, FFN_PASSES, PASSES_PER_QUANTISE):
                 gs = slice(g0, g0 + PASSES_PER_QUANTISE)
                 nc.vector.quantize_mx(
                     out=act_codes[:, m, gs, :].bitcast(FP8X4).rearrange("p g r -> p (g r)"),
                     scales=act_scales[:, m, gs, :].rearrange("p g r -> p (g r)"),
-                    in_=act_grouped[:, gs, :].rearrange("p g c -> p (g c)"),
+                    in_=grouped_acts[m][:, gs, :].rearrange("p g c -> p (g c)"),
                 )
 
         gain_all = keep.tile([P, E], BF16)
         for m in range(TOKEN_TILES):
             prepare_act(m)
+            if m < TOKEN_TILES - 1:
+                quantise_act(m)
             if m == 0:
                 gain_ps = psum.tile([P, E], BF16, tag="bank")
                 for half in range(E_HALVES):
                     cols = slice(half * BANK, (half + 1) * BANK)
                     nc.tensor.matmul(out=gain_ps[:, cols], lhsT=ones[:], rhs=gain_rows[:, cols], start=True, stop=True)
-                nc.vector.tensor_copy(out=gain_all[:], in_=gain_ps[:])
+                nc.scalar.copy(out=gain_all[:], in_=gain_ps[:])
 
         acc = {}
         for m in range(TOKEN_TILES):
@@ -171,17 +177,19 @@ def tile_textencoderblock_pc_kernel(tc, ffn_act, wd, residual, ln1_w, wk, wv, ou
                 regroup(copy, wd_raw[c][:, :, half * BANK : (half + 1) * BANK], grouped_tile(c, half)[:])
             if c + WD_BUFS < FFN_PASSES:
                 load_wd(c + WD_BUFS)
+            if c == 0:
+                quantise_act(TOKEN_TILES - 1)
             if c > 0:
                 quantise_and_multiply(c - 1, 1)
             quantise_and_multiply(c, 0)
         c = FFN_PASSES - 1
-        regroup(nc.vector.tensor_copy, wd_raw[c][:, :, 0:BANK], grouped_tile(c, 0)[:])
-        quantise_and_multiply(c - 1, 1)
-        quantise_and_multiply(c, 0)
-        last = grouped_tile(c, 1)
-        shared = BANK // 2
-        regroup(nc.vector.tensor_copy, wd_raw[c][:, :, BANK : BANK + shared], last[:, 0:shared, :])
-        regroup(nc.scalar.copy, wd_raw[c][:, :, BANK + shared : E], last[:, shared:BANK, :])
+        for half in range(E_HALVES):
+            grouped = grouped_tile(c, half)
+            for copy, n0, n1 in ((nc.vector.tensor_copy, 0, BANK // 2), (nc.scalar.copy, BANK // 2, BANK)):
+                regroup(copy, wd_raw[c][:, :, half * BANK + n0 : half * BANK + n1], grouped[:, n0:n1, :])
+            if half == 0:
+                quantise_and_multiply(c - 1, 1)
+                quantise_and_multiply(c, 0)
 
         wkv_raw = []
         res_all = keep.tile([P, TOKEN_TILES, E], BF16)

@@ -215,6 +215,7 @@ def tile_textencoderblock_pc_kernel(tc, ffn_act, wd, residual, ln1_w, wk, wv, ou
         regroup_wkv(0, 1)
 
         x_sb = []
+        squares_sb = []
         sum_sq = []
         inv_rms = []
 
@@ -226,10 +227,18 @@ def tile_textencoderblock_pc_kernel(tc, ffn_act, wd, residual, ln1_w, wk, wv, ou
 
         def measure(m):
             nc.sync.dma_start(out=x_rows[m * P : (m + 1) * P, :], in_=x_sb[m][:])
-            squares = tail.tile([P, E], BF16, tag="squares")
+            squares = tail.tile([P, E], BF16, tag="squares", bufs=TOKEN_TILES, name="squares_%d" % m)
             total = tail.tile([P, 1], F32, tag="sum_sq", bufs=TOKEN_TILES, name="sum_sq_%d" % m)
             nc.scalar.activation(out=squares[:], in_=x_sb[m][:], func=ACT.Square, accum_out=total[:])
             sum_sq.append(total)
+            squares_sb.append(squares)
+
+        def keep_busy(tile, halves):
+            unread = psum.tile([P, BANK], F32, tag="bank", name="unread")
+            for half in range(halves):
+                nc.tensor.matmul(
+                    out=unread[:], lhsT=ones[:], rhs=tile[:, half * BANK : (half + 1) * BANK], start=True, stop=True
+                )
 
         def invert(m):
             inv = tail.tile([P, 1], F32, tag="inv_rms", bufs=TOKEN_TILES, name="inv_rms_%d" % m)
@@ -247,10 +256,12 @@ def tile_textencoderblock_pc_kernel(tc, ffn_act, wd, residual, ln1_w, wk, wv, ou
         invert(TOKEN_TILES - 1)
         regroup_wkv(1, 1)
 
+        h_sb = []
         h_grouped = []
 
         def normalise(m):
-            h = tail.tile([P, E], BF16, tag="h")
+            h = tail.tile([P, E], BF16, tag="h", bufs=TOKEN_TILES, name="h_%d" % m)
+            h_sb.append(h)
             nc.vector.scalar_tensor_tensor(
                 out=h[:], in0=x_sb[m][:], scalar=inv_rms[m][:], in1=gain_all[:], op0=ALU.mult, op1=ALU.mult
             )
@@ -307,10 +318,16 @@ def tile_textencoderblock_pc_kernel(tc, ffn_act, wd, residual, ln1_w, wk, wv, ou
             nc.sync.dma_start(out=k_rows[m * P : (m + 1) * P, :], in_=kv[:, 0:KV])
             nc.sync.dma_start(out=v_rows[m * P : (m + 1) * P, :], in_=kv[:, KV : 2 * KV])
 
+        keep_busy(squares_sb[0], 2)
+        keep_busy(squares_sb[1], 2)
         normalise(0)
+        keep_busy(squares_sb[2], 2)
         normalise(1)
+        keep_busy(squares_sb[3], 2)
+        keep_busy(h_sb[1], 2)
         quantise_wkv(0)
         normalise(2)
+        keep_busy(h_sb[2], 1)
         quantise_wkv(1)
         quantise_h(0)
         project(0)

from contextlib import ExitStack

import concourse.mybir as mybir
from concourse.masks import make_identity

F32 = mybir.dt.float32
BF16 = mybir.dt.bfloat16
U32 = mybir.dt.uint32
U8 = mybir.dt.uint8
FP8X4 = mybir.dt.float8_e4m3fn_x4
ALU = mybir.AluOpType
ACT = mybir.ActivationFunctionType

P = 128
PACK = 4
K_PASS = P * PACK
BANK = 512
BANKS = 8

TOKENS = 512
FFN = 4096
E = 1024
KV = 256
EPS = 2.0 ** -23

TOKEN_TILES = TOKENS // P
FFN_PASSES = FFN // K_PASS
E_PASSES = E // K_PASS
E_HALVES = E // BANK
PASSES_PER_BANK = 2
PASSES_PER_QUANTISE = 4
RUN = 4
WD_BUFS = 6

FLOPS = 2 * TOKENS * FFN * E + 2 * TOKENS * E * 2 * KV


def regroup(copy, four_rows, grouped):
    copy(
        out=grouped.rearrange("p (c i) t -> p c t i", i=RUN),
        in_=four_rows.rearrange("p t (c i) -> p c t i", i=RUN),
    )


def tile_textencoderblock_pc_kernel(tc, ffn_act, wd, residual, ln1_w, wk, wv, out_0, out_1, out_2):
    nc = tc.nc
    act_rows = ffn_act.flatten_outer_dims()
    res_rows = residual.flatten_outer_dims()
    x_rows = out_0.flatten_outer_dims()
    k_rows = out_1.flatten_outer_dims()
    v_rows = out_2.flatten_outer_dims()

    with ExitStack() as ctx:
        keep = ctx.enter_context(tc.tile_pool(name="keep", bufs=1))
        act_pool = ctx.enter_context(tc.tile_pool(name="act", bufs=2))
        wd_pool = ctx.enter_context(tc.tile_pool(name="wd", bufs=3))
        tail = ctx.enter_context(tc.tile_pool(name="tail", bufs=2))
        psum = ctx.enter_context(tc.psum_pool(name="psum", bufs=BANKS))
        ctx.enter_context(tc.manual_schedule())

        gain_rows = keep.tile([P, E], BF16)
        nc.vector.memset(gain_rows[:], 0.0)
        ones = keep.tile([P, P], BF16)
        nc.vector.memset(ones[:], 1.0)
        one_col = keep.tile([P, 1], F32)
        nc.vector.memset(one_col[:], 1.0)
        warm_col = keep.tile([P, 1], F32)
        nc.scalar.activation(out=warm_col[:], in_=one_col[:], func=ACT.Abs_reciprocal_sqrt)
        ident_f32 = keep.tile([P, P], F32)
        make_identity(nc, ident_f32[:])

        act_raw = []
        for m in range(TOKEN_TILES):
            raw = act_pool.tile([P, FFN], BF16, tag="act_raw", bufs=TOKEN_TILES, name="act_raw_%d" % m)
            nc.sync.dma_start(out=raw[:], in_=act_rows[m * P : (m + 1) * P, :])
            act_raw.append(raw)
            if m == 0:
                nc.sync.dma_start(out=gain_rows[0:1, :], in_=ln1_w.rearrange("(o e) -> o e", o=1))

        wd_raw = {}

        def load_wd(c):
            raw = wd_pool.tile([P, PACK, E], BF16, tag="wd_raw", bufs=WD_BUFS, name="wd_raw_%d" % c)
            rows = wd[c * K_PASS : (c + 1) * K_PASS, :]
            if c < FFN_PASSES - 1:
                nc.sync.dma_start(
                    out=raw[:].rearrange("p (u e) n -> p u e n", u=2),
                    in_=rows.rearrange("(u p e) n -> p u e n", u=2, e=2),
                )
            else:
                for half in range(E_HALVES):
                    cols = slice(half * BANK, (half + 1) * BANK)
                    for u in range(2):
                        nc.sync.dma_start(
                            out=raw[:, 2 * u : 2 * u + 2, cols],
                            in_=rows[u * 2 * P : (u + 1) * 2 * P, cols].rearrange("(p e) n -> p e n", e=2),
                        )
            wd_raw[c] = raw

        for c in range(WD_BUFS):
            load_wd(c)

        act_codes = keep.tile([P, TOKEN_TILES, FFN_PASSES, P], U32, align_bytes=64)
        act_scales = keep.tile([P, TOKEN_TILES, FFN_PASSES, P], U8, align_bytes=64)

        grouped_acts = []

        def prepare_act(m):
            act_words = act_raw[m][:].bitcast(F32)
            act_grouped = act_pool.tile([P, FFN_PASSES, P * PACK], BF16, tag="act_grouped", align_bytes=64)
            grouped_words = act_grouped[:].bitcast(F32).rearrange("p g (r u) -> p g r u", u=2)
            for g0 in range(0, FFN_PASSES, PASSES_PER_BANK):
                words_t = psum.tile([P, PASSES_PER_BANK, 2, P], F32, tag="bank")
                for j in range(PASSES_PER_BANK):
                    for u in range(2):
                        w0 = (g0 + j) * 2 * P + u * P
                        nc.tensor.transpose(words_t[:, j, u, :], act_words[:, w0 : w0 + P], ident_f32[:])
                nc.scalar.copy(
                    out=grouped_words[:, g0 : g0 + PASSES_PER_BANK],
                    in_=words_t[:].rearrange("p g u r -> p g r u"),
                )
            grouped_acts.append(act_grouped)

        def quantise_act(m):
            for g0 in range(0, FFN_PASSES, PASSES_PER_QUANTISE):
                gs = slice(g0, g0 + PASSES_PER_QUANTISE)
                nc.vector.quantize_mx(
                    out=act_codes[:, m, gs, :].bitcast(FP8X4).rearrange("p g r -> p (g r)"),
                    scales=act_scales[:, m, gs, :].rearrange("p g r -> p (g r)"),
                    in_=grouped_acts[m][:, gs, :].rearrange("p g c -> p (g c)"),
                )

        gain_all = keep.tile([P, E], BF16)
        for m in range(TOKEN_TILES):
            prepare_act(m)
            if m < TOKEN_TILES - 1:
                quantise_act(m)
            if m == 0:
                gain_ps = psum.tile([P, E], BF16, tag="bank")
                for half in range(E_HALVES):
                    cols = slice(half * BANK, (half + 1) * BANK)
                    nc.tensor.matmul(out=gain_ps[:, cols], lhsT=ones[:], rhs=gain_rows[:, cols], start=True, stop=True)
                nc.scalar.copy(out=gain_all[:], in_=gain_ps[:])

        acc = {}
        for m in range(TOKEN_TILES):
            for half in range(E_HALVES):
                acc[(m, half)] = psum.tile([P, BANK], F32, tag="bank", name="acc_%d_%d" % (m, half))

        wd_grouped = {}

        def quantise_and_multiply(c, half):
            codes = wd_pool.tile([P, BANK], U32, tag="wd_codes", align_bytes=64)
            scales = wd_pool.tile([P, BANK], U8, tag="wd_scales", align_bytes=64)
            nc.vector.quantize_mx(
                out=codes[:].bitcast(FP8X4),
                scales=scales[:],
                in_=wd_grouped[(c, half)][:].rearrange("p n t -> p (n t)"),
            )
            for m in range(TOKEN_TILES):
                nc.tensor.matmul_mx(
                    out=acc[(m, half)][:],
                    lhsT=act_codes[:, m, c, :].bitcast(FP8X4),
                    lhsT_scale=act_scales[:, m, c, :],
                    rhs=codes[:].bitcast(FP8X4),
                    rhs_scale=scales[:],
                    start=(c == 0),
                    stop=(c == FFN_PASSES - 1),
                )

        def grouped_tile(c, half):
            wd_grouped[(c, half)] = wd_pool.tile([P, BANK, PACK], BF16, tag="wd_grouped_%d" % half, align_bytes=64, name="wd_grouped_%d_%d" % (c, half))
            return wd_grouped[(c, half)]

        for c in range(FFN_PASSES - 1):
            for half, copy in enumerate((nc.vector.tensor_copy, nc.scalar.copy)):
                regroup(copy, wd_raw[c][:, :, half * BANK : (half + 1) * BANK], grouped_tile(c, half)[:])
            if c + WD_BUFS < FFN_PASSES:
                load_wd(c + WD_BUFS)
            if c == 0:
                quantise_act(TOKEN_TILES - 1)
            if c > 0:
                quantise_and_multiply(c - 1, 1)
            quantise_and_multiply(c, 0)
        c = FFN_PASSES - 1
        for half in range(E_HALVES):
            grouped = grouped_tile(c, half)
            for copy, n0, n1 in ((nc.vector.tensor_copy, 0, BANK // 2), (nc.scalar.copy, BANK // 2, BANK)):
                regroup(copy, wd_raw[c][:, :, half * BANK + n0 : half * BANK + n1], grouped[:, n0:n1, :])
            if half == 0:
                quantise_and_multiply(c - 1, 1)
                quantise_and_multiply(c, 0)

        wkv_raw = []
        res_all = keep.tile([P, TOKEN_TILES, E], BF16)
        for i, weight in enumerate((wk, wv)):
            raw = keep.tile([P, E_PASSES, PACK, KV], BF16, name="w%s_raw" % "kv"[i])
            nc.sync.dma_start(
                out=raw[:].rearrange("p g (u j) n -> p (g u) j n", j=2),
                in_=weight.rearrange("(v p j) n -> p v j n", p=P, j=2),
            )
            wkv_raw.append(raw)
            for m in (2 * i, 2 * i + 1):
                nc.sync.dma_start(out=res_all[:, m, :], in_=res_rows[m * P : (m + 1) * P, :])

        quantise_and_multiply(FFN_PASSES - 1, 1)

        wkv_grouped = keep.tile([P, E_PASSES, 2 * KV, PACK], BF16, align_bytes=64)

        def regroup_wkv(g, i):
            regroup(nc.scalar.copy, wkv_raw[i][:, g], wkv_grouped[:, g, i * KV : (i + 1) * KV])

        regroup_wkv(0, 0)
        regroup_wkv(1, 0)
        regroup_wkv(0, 1)

        x_sb = []
        squares_sb = []
        sum_sq = []
        inv_rms = []

        def add_residual(m, half):
            if half == 0:
                x_sb.append(tail.tile([P, E], F32, tag="x", bufs=TOKEN_TILES, name="x_%d" % m))
            cols = slice(half * BANK, (half + 1) * BANK)
            nc.vector.tensor_tensor(out=x_sb[m][:, cols], in0=acc[(m, half)][:], in1=res_all[:, m, cols], op=ALU.add)

        def measure(m):
            nc.sync.dma_start(out=x_rows[m * P : (m + 1) * P, :], in_=x_sb[m][:])
            squares = tail.tile([P, E], BF16, tag="squares", bufs=TOKEN_TILES, name="squares_%d" % m)
            total = tail.tile([P, 1], F32, tag="sum_sq", bufs=TOKEN_TILES, name="sum_sq_%d" % m)
            nc.scalar.activation(out=squares[:], in_=x_sb[m][:], func=ACT.Square, accum_out=total[:])
            sum_sq.append(total)
            squares_sb.append(squares)

        def keep_busy(tile, halves):
            unread = psum.tile([P, BANK], F32, tag="bank", name="unread")
            for half in range(halves):
                nc.tensor.matmul(
                    out=unread[:], lhsT=ones[:], rhs=tile[:, half * BANK : (half + 1) * BANK], start=True, stop=True
                )

        def invert(m):
            inv = tail.tile([P, 1], F32, tag="inv_rms", bufs=TOKEN_TILES, name="inv_rms_%d" % m)
            nc.scalar.activation(out=inv[:], in_=sum_sq[m][:], func=ACT.Abs_reciprocal_sqrt, scale=1.0 / E, bias=EPS)
            inv_rms.append(inv)

        for m in (0, 2):
            for half in range(E_HALVES):
                add_residual(m, half)
                add_residual(m + 1, half)
            for i in (m, m + 1):
                measure(i)
                if i > 0:
                    invert(i - 1)
        invert(TOKEN_TILES - 1)
        regroup_wkv(1, 1)

        h_sb = []
        h_grouped = []

        def normalise(m):
            h = tail.tile([P, E], BF16, tag="h", bufs=TOKEN_TILES, name="h_%d" % m)
            h_sb.append(h)
            nc.vector.scalar_tensor_tensor(
                out=h[:], in0=x_sb[m][:], scalar=inv_rms[m][:], in1=gain_all[:], op0=ALU.mult, op1=ALU.mult
            )
            h_words = h[:].bitcast(F32)
            h_t = psum.tile([P, E_PASSES, 2, P], F32, tag="bank")
            for g in range(E_PASSES):
                for u in range(2):
                    w0 = g * 2 * P + u * P
                    nc.tensor.transpose(h_t[:, g, u, :], h_words[:, w0 : w0 + P], ident_f32[:])
            grouped = tail.tile([P, E_PASSES, P * PACK], BF16, tag="h_grouped", bufs=TOKEN_TILES, align_bytes=64, name="h_grouped_%d" % m)
            nc.scalar.copy(
                out=grouped[:].bitcast(F32).rearrange("p g (r u) -> p g r u", u=2),
                in_=h_t[:].rearrange("p g u r -> p g r u"),
            )
            h_grouped.append(grouped)

        wkv_codes = keep.tile([P, E_PASSES, 2 * KV], U32, align_bytes=64)
        wkv_scales = keep.tile([P, E_PASSES, 2 * KV], U8, align_bytes=64)

        def quantise_wkv(g):
            nc.vector.quantize_mx(
                out=wkv_codes[:, g, :].bitcast(FP8X4),
                scales=wkv_scales[:, g, :],
                in_=wkv_grouped[:, g].rearrange("p n t -> p (n t)"),
            )

        h_quantised = []

        def quantise_h(m):
            codes = tail.tile([P, E_PASSES, P], U32, tag="h_codes", bufs=TOKEN_TILES, align_bytes=64, name="h_codes_%d" % m)
            scales = tail.tile([P, E_PASSES, P], U8, tag="h_scales", bufs=TOKEN_TILES, align_bytes=64, name="h_scales_%d" % m)
            nc.vector.quantize_mx(
                out=codes[:].bitcast(FP8X4).rearrange("p g r -> p (g r)"),
                scales=scales[:].rearrange("p g r -> p (g r)"),
                in_=h_grouped[m][:].rearrange("p g c -> p (g c)"),
            )
            h_quantised.append((codes, scales))

        def project(m):
            h_codes, h_scales = h_quantised[m]
            kv_ps = psum.tile([P, 2 * KV], F32, tag="bank")
            for g in range(E_PASSES):
                nc.tensor.matmul_mx(
                    out=kv_ps[:],
                    lhsT=h_codes[:, g, :].bitcast(FP8X4),
                    lhsT_scale=h_scales[:, g, :],
                    rhs=wkv_codes[:, g, :].bitcast(FP8X4),
                    rhs_scale=wkv_scales[:, g, :],
                    start=(g == 0),
                    stop=(g == E_PASSES - 1),
                )
            kv = tail.tile([P, 2 * KV], F32, tag="kv", bufs=TOKEN_TILES)
            nc.scalar.copy(out=kv[:], in_=kv_ps[:])
            nc.sync.dma_start(out=k_rows[m * P : (m + 1) * P, :], in_=kv[:, 0:KV])
            nc.sync.dma_start(out=v_rows[m * P : (m + 1) * P, :], in_=kv[:, KV : 2 * KV])

        keep_busy(squares_sb[0], 2)
        keep_busy(squares_sb[1], 2)
        normalise(0)
        keep_busy(squares_sb[2], 2)
        normalise(1)
        keep_busy(squares_sb[3], 2)
        keep_busy(h_sb[1], 2)
        quantise_wkv(0)
        normalise(2)
        keep_busy(h_sb[2], 1)
        quantise_wkv(1)
        quantise_h(0)
        project(0)
        normalise(3)
        quantise_h(1)
        project(1)
        quantise_h(2)
        project(2)
        quantise_h(3)
        project(3)
